import numpy as np
import ml_dtypes


def mxq(x, axis, fmt="e4m3"):
    dtype, down = {"e4m3": (ml_dtypes.float8_e4m3fn, 7), "e5m2": (ml_dtypes.float8_e5m2, 14)}[fmt]
    v = np.moveaxis(np.asarray(x, np.float32).astype(ml_dtypes.bfloat16).astype(np.float64), axis, -1)
    blocks = v.reshape(v.shape[:-1] + (-1, 32))
    amax = np.abs(blocks).max(-1, keepdims=True)
    byte = np.maximum(np.where(amax > 0, np.frexp(amax)[1] - 1 + 127, 0) - down, 1)
    scale = np.exp2(byte - 127.0)
    codes = (blocks / scale).astype(np.float32).astype(dtype).astype(np.float64)
    return np.moveaxis((codes * scale).reshape(v.shape), -1, axis)


WIDE = False


def mx_kscale(k):
    if not WIDE:
        return np.ones(k)
    levels = np.array([10, -10, 5, -5, 0])
    a = np.random.permutation(np.resize(levels, k // 512 * 4)).reshape(k // 512, 4)
    idx = np.arange(k)
    return np.exp2(a[idx // 512, idx % 128 // 32])


BF16 = ml_dtypes.bfloat16


def bf(x):
    return np.asarray(x, np.float32).astype(BF16)


def f64(x):
    return np.asarray(x).astype(np.float64)


B, C_IN, C_OUT, K, H, W = 2, 512, 512, 3, 16, 32


def _shift2d(x, dh, dw):
    hh, ww = x.shape[2], x.shape[3]
    ph, pw = abs(dh), abs(dw)
    xp = np.pad(x, ((0, 0), (0, 0), (ph, ph), (pw, pw)))
    return xp[:, :, ph + dh: ph + dh + hh, pw + dw: pw + dw + ww]


def setup_inputs():
    s = mx_kscale(C_IN)
    bound = np.sqrt(2.0) * np.sqrt(3.0 / (C_IN * K))
    return {"x": bf(np.random.standard_normal((B, C_IN, H, W)) * s[None, :, None, None]),
            "weight": bf(np.random.uniform(-bound, bound, (C_OUT, C_IN, K)) / s[None, :, None]),
            "dilation": 1, "step": 1}


def reference(x, weight, dilation, step):
    nb, nc_in, nh, nw = x.shape
    no, nk = weight.shape[0], weight.shape[2]
    c0 = nk // 2
    xq = mxq(f64(x).reshape(nb, nc_in, nh * nw), 1, "e4m3")
    out = np.zeros((nb, no, nh, nw))
    for k in range(nk):
        off = k - c0
        y = mxq(f64(weight)[:, :, k], 1, "e4m3") @ xq
        out = out + _shift2d(y.reshape(nb, no, nh, nw), off * step, off * dilation)
    return out

@@ -1,0 +1,163 @@
+from contextlib import ExitStack
+
+import concourse.bass as bass
+import concourse.mybir as mybir
+import concourse.tile as tile
+from concourse.masks import make_identity
+
+FLOPS = 2 * 2 * 512 * 512 * 3 * 512
+
+BF16 = mybir.dt.bfloat16
+F32 = mybir.dt.float32
+I32 = mybir.dt.int32
+U32 = mybir.dt.uint32
+U8 = mybir.dt.uint8
+FP8X4 = mybir.dt.float8_e4m3fn_x4
+
+P = 128
+NB = 2
+H = 16
+W = 32
+TAPS = 3
+NOT = 4
+PITCH = 35
+ROWS = 33
+COLS = 1152
+SHIFT = PITCH + 1
+THIRD = 384
+RPT = 11
+
+
+def tile_skeletonconv_kernel(tc, x, weight, dilation, step, out):
+    nc = tc.nc
+    assert dilation == 1 and step == 1
+    with ExitStack() as ctx:
+        keep = ctx.enter_context(tc.tile_pool(name="keep", bufs=1))
+        outs = ctx.enter_context(tc.tile_pool(name="outs", bufs=4))
+        pst = ctx.enter_context(tc.psum_pool(name="pst", bufs=3))
+        psa = ctx.enter_context(tc.psum_pool(name="psa", bufs=5))
+
+        ident = keep.tile([P, P], F32, name="ident")
+        w_raw = [keep.tile([P, 1536], BF16, name="w_raw%d" % a) for a in range(NOT)]
+        w_tap = [keep.tile([P, 1536], BF16, name="w_tap%d" % a) for a in range(NOT)]
+        w_grp = keep.tile([P, 12 * 512], BF16, name="w_grp", align_bytes=64)
+        w_cod = keep.tile([P, 12 * P], U32, name="w_cod", align_bytes=64)
+        w_scl = keep.tile([P, 12 * P], U8, name="w_scl", align_bytes=64)
+        x_raw = [keep.tile([P, 4, 512], BF16, name="x_raw%d" % b) for b in range(NB)]
+        x_grp = keep.tile([P, 1160 * 4], BF16, name="x_grp", align_bytes=64)
+        x_cod = [keep.tile([P, COLS], U32, name="x_cod%d" % t, align_bytes=64) for t in range(TAPS)]
+        x_scl = [keep.tile([P, COLS], U8, name="x_scl%d" % t, align_bytes=64) for t in range(TAPS)]
+
+        w_view = weight.rearrange("(a p) c t -> a p (c t)", p=P)
+        nc.sync.dma_start(out=w_raw[0][:], in_=w_view[0])
+        for b in range(NB):
+            nc.sync.dma_start(
+                out=x_raw[b][:].rearrange("p (u e) n -> p u (e n)", u=2),
+                in_=x[b].rearrange("(u p e) h w -> p u (e h w)", u=2, p=P, e=2),
+            )
+        for a in range(1, NOT):
+            nc.sync.dma_start(out=w_raw[a][:], in_=w_view[a])
+
+        make_identity(nc, ident[:])
+        nc.vector.memset(x_grp[:].bitcast(I32), 0)
+        nc.vector.memset(x_scl[1][:].bitcast(I32), 0)
+        nc.vector.memset(x_cod[0][:, 0:SHIFT].bitcast(I32), 0)
+        nc.vector.memset(x_cod[2][:, COLS - SHIFT:COLS].bitcast(I32), 0)
+        nc.vector.memset(x_scl[0][:, 0:SHIFT].bitcast(I32), 0)
+        nc.vector.memset(x_scl[2][:, COLS - SHIFT:COLS].bitcast(I32), 0)
+
+        w_grp32 = w_grp[:].bitcast(F32).rearrange("p (n o u) -> p n o u", n=12, u=2)
+
+        def w_split(a):
+            nc.vector.tensor_copy(
+                out=w_tap[a][:].rearrange("p (t c) -> p t c", t=TAPS),
+                in_=w_raw[a][:].rearrange("p (c t) -> p t c", t=TAPS),
+            )
+
+        def w_pair(k):
+            pt = pst.tile([P, 2, 2, P], F32, name="pt")
+            for i in range(2):
+                a, t = divmod(2 * k + i, TAPS)
+                words = w_tap[a][:].bitcast(F32)
+                for u in range(2):
+                    c0 = 256 * t + P * u
+                    nc.tensor.transpose(pt[:, i, u, :], words[:, c0:c0 + P], ident[:])
+            nc.scalar.copy(out=w_grp32[:, 2 * k:2 * k + 2, :, :], in_=pt[:].rearrange("p i u o -> p i o u"))
+            nc.vector.quantize_mx(
+                out=w_cod[:, 256 * k:256 * (k + 1)].bitcast(FP8X4),
+                scales=w_scl[:, 256 * k:256 * (k + 1)],
+                in_=w_grp[:, 1024 * k:1024 * (k + 1)],
+            )
+
+        x_cols = x_grp[:].rearrange("p (n j) -> p n j", j=4)
+
+        def x_group(b):
+            base = 17 * PITCH * b
+            dst = x_cols[:, base:base + H * PITCH, :].rearrange("p (h q) j -> p h q j", q=PITCH)[:, :, 0:W, :]
+            nc.vector.tensor_copy(
+                out=dst.rearrange("p h (c i) j -> p h c j i", i=4),
+                in_=x_raw[b][:].rearrange("p j (h c i) -> p h c j i", h=H, i=4),
+            )
+
+        def x_quant(c0, n):
+            nc.vector.quantize_mx(
+                out=x_cod[1][:, c0:c0 + n].bitcast(FP8X4),
+                scales=x_scl[1][:, c0:c0 + n],
+                in_=x_grp[:, 4 * c0:4 * (c0 + n)],
+            )
+
+        def x_move():
+            n = COLS - SHIFT
+            nc.vector.tensor_copy(out=x_cod[0][:, SHIFT:COLS].bitcast(I32), in_=x_cod[1][:, 0:n].bitcast(I32))
+            nc.vector.tensor_copy(out=x_scl[0][:, SHIFT:COLS].bitcast(I32), in_=x_scl[1][:, 0:n].bitcast(I32))
+            nc.vector.tensor_copy(out=x_cod[2][:, 0:n].bitcast(I32), in_=x_cod[1][:, SHIFT:COLS].bitcast(I32))
+            nc.vector.tensor_copy(out=x_scl[2][:, 0:n].bitcast(I32), in_=x_scl[1][:, SHIFT:COLS].bitcast(I32))
+
+        w_split(0)
+        x_group(0)
+        x_group(1)
+        x_quant(0, 512)
+        x_quant(512, 512)
+        x_quant(1024, 128)
+        x_move()
+        w_pair(0)
+        w_split(1)
+        w_pair(1)
+        w_pair(2)
+        w_split(2)
+        w_pair(3)
+        w_split(3)
+        w_pair(4)
+        w_pair(5)
+
+        n_exit = 0
+        for a in range(NOT):
+            res = outs.tile([P, ROWS, W], F32, name="res")
+            for k in range(3):
+                acc = psa.tile([P, 512], F32, name="acc")
+                for n0, n in ((0, 256), (256, 128)):
+                    c0 = THIRD * k + n0
+                    for i, t in enumerate((1, 0, 2)):
+                        un = TAPS * a + t
+                        nc.tensor.matmul_mx(
+                            out=acc[:, n0:n0 + n],
+                            lhsT=w_cod[:, P * un:P * (un + 1)].bitcast(FP8X4),
+                            lhsT_scale=w_scl[:, P * un:P * (un + 1)],
+                            rhs=x_cod[t][:, c0:c0 + n].bitcast(FP8X4),
+                            rhs_scale=x_scl[t][:, c0:c0 + n],
+                            start=(i == 0),
+                            stop=(i == 2),
+                        )
+                src = acc[:, k:k + RPT * PITCH].rearrange("p (r q) -> p r q", q=PITCH)[:, :, 0:W]
+                dst = res[:, RPT * k:RPT * (k + 1), :]
+                if n_exit % 2 == 0:
+                    nc.vector.tensor_copy(out=dst, in_=src)
+                else:
+                    nc.scalar.copy(out=dst, in_=src)
+                n_exit += 1
+                if k >= 1:
+                    b = k - 1
+                    nc.sync.dma_start(
+                        out=out[b, P * a:P * (a + 1)].rearrange("o h w -> o (h w)"),
+                        in_=res[:, 17 * b:17 * b + H, :].rearrange("p r w -> p (r w)"),
+                    )

@@ -1,8 +1,6 @@
 from contextlib import ExitStack
 
-import concourse.bass as bass
 import concourse.mybir as mybir
-import concourse.tile as tile
 from concourse.masks import make_identity
 
 FLOPS = 2 * 2 * 512 * 512 * 3 * 512
@@ -33,61 +31,67 @@ def tile_skeletonconv_kernel(tc, x, weight, dilation, step, out):
     assert dilation == 1 and step == 1
     with ExitStack() as ctx:
         keep = ctx.enter_context(tc.tile_pool(name="keep", bufs=1))
-        outs = ctx.enter_context(tc.tile_pool(name="outs", bufs=4))
         pst = ctx.enter_context(tc.psum_pool(name="pst", bufs=3))
         psa = ctx.enter_context(tc.psum_pool(name="psa", bufs=5))
 
         ident = keep.tile([P, P], F32, name="ident")
         w_raw = [keep.tile([P, 1536], BF16, name="w_raw%d" % a) for a in range(NOT)]
         w_tap = [keep.tile([P, 1536], BF16, name="w_tap%d" % a) for a in range(NOT)]
-        w_grp = keep.tile([P, 12 * 512], BF16, name="w_grp", align_bytes=64)
-        w_cod = keep.tile([P, 12 * P], U32, name="w_cod", align_bytes=64)
-        w_scl = keep.tile([P, 12 * P], U8, name="w_scl", align_bytes=64)
+        w_grp = [keep.tile([P, 1536], BF16, name="w_grp%d" % a, align_bytes=64) for a in range(NOT)]
+        w_cod = [keep.tile([P, TAPS * P], U32, name="w_cod%d" % a, align_bytes=64) for a in range(NOT)]
+        w_scl = [keep.tile([P, TAPS * P], U8, name="w_scl%d" % a, align_bytes=64) for a in range(NOT)]
         x_raw = [keep.tile([P, 4, 512], BF16, name="x_raw%d" % b) for b in range(NB)]
         x_grp = keep.tile([P, 1160 * 4], BF16, name="x_grp", align_bytes=64)
         x_cod = [keep.tile([P, COLS], U32, name="x_cod%d" % t, align_bytes=64) for t in range(TAPS)]
         x_scl = [keep.tile([P, COLS], U8, name="x_scl%d" % t, align_bytes=64) for t in range(TAPS)]
+        res = [keep.tile([P, ROWS, W], F32, name="res%d" % a) for a in range(NOT)]
 
         w_view = weight.rearrange("(a p) c t -> a p (c t)", p=P)
-        nc.sync.dma_start(out=w_raw[0][:], in_=w_view[0])
-        for b in range(NB):
+
+        def load_w(a):
+            nc.sync.dma_start(out=w_raw[a][:], in_=w_view[a])
+
+        def load_x(b):
             nc.sync.dma_start(
                 out=x_raw[b][:].rearrange("p (u e) n -> p u (e n)", u=2),
                 in_=x[b].rearrange("(u p e) h w -> p u (e h w)", u=2, p=P, e=2),
             )
-        for a in range(1, NOT):
-            nc.sync.dma_start(out=w_raw[a][:], in_=w_view[a])
 
-        make_identity(nc, ident[:])
-        nc.vector.memset(x_grp[:].bitcast(I32), 0)
-        nc.vector.memset(x_scl[1][:].bitcast(I32), 0)
-        nc.vector.memset(x_cod[0][:, 0:SHIFT].bitcast(I32), 0)
-        nc.vector.memset(x_cod[2][:, COLS - SHIFT:COLS].bitcast(I32), 0)
-        nc.vector.memset(x_scl[0][:, 0:SHIFT].bitcast(I32), 0)
-        nc.vector.memset(x_scl[2][:, COLS - SHIFT:COLS].bitcast(I32), 0)
+        def zeros():
+            make_identity(nc, ident[:])
+            nc.vector.memset(x_grp[:].bitcast(I32), 0)
+            nc.vector.memset(x_scl[1][:].bitcast(I32), 0)
+            nc.vector.memset(x_cod[0][:, 0:SHIFT].bitcast(I32), 0)
+            nc.vector.memset(x_cod[2][:, COLS - SHIFT:COLS].bitcast(I32), 0)
+            nc.vector.memset(x_scl[0][:, 0:SHIFT].bitcast(I32), 0)
+            nc.vector.memset(x_scl[2][:, COLS - SHIFT:COLS].bitcast(I32), 0)
 
-        w_grp32 = w_grp[:].bitcast(F32).rearrange("p (n o u) -> p n o u", n=12, u=2)
+        def w_split(a, eng):
+            dst = w_tap[a][:].rearrange("p (t c) -> p t c", t=TAPS)
+            src = w_raw[a][:].rearrange("p (c t) -> p t c", t=TAPS)
+            if eng == "v":
+                nc.vector.tensor_copy(out=dst, in_=src)
+            else:
+                nc.scalar.copy(out=dst, in_=src)
 
-        def w_split(a):
-            nc.vector.tensor_copy(
-                out=w_tap[a][:].rearrange("p (t c) -> p t c", t=TAPS),
-                in_=w_raw[a][:].rearrange("p (c t) -> p t c", t=TAPS),
-            )
+        def w_turn(a):
+            words = w_tap[a][:].bitcast(F32)
+            grp32 = w_grp[a][:].bitcast(F32).rearrange("p (t o u) -> p t o u", t=TAPS, u=2)
+            for t0, nt in ((0, 2), (2, 1)):
+                pt = pst.tile([P, 2, 2, P], F32, name="pt")
+                for i in range(nt):
+                    for u in range(2):
+                        c0 = 256 * (t0 + i) + P * u
+                        nc.tensor.transpose(pt[:, i, u, :], words[:, c0:c0 + P], ident[:])
+                nc.scalar.copy(out=grp32[:, t0:t0 + nt, :, :], in_=pt[:, 0:nt, :, :].rearrange("p i u o -> p i o u"))
 
-        def w_pair(k):
-            pt = pst.tile([P, 2, 2, P], F32, name="pt")
-            for i in range(2):
-                a, t = divmod(2 * k + i, TAPS)
-                words = w_tap[a][:].bitcast(F32)
-                for u in range(2):
-                    c0 = 256 * t + P * u
-                    nc.tensor.transpose(pt[:, i, u, :], words[:, c0:c0 + P], ident[:])
-            nc.scalar.copy(out=w_grp32[:, 2 * k:2 * k + 2, :, :], in_=pt[:].rearrange("p i u o -> p i o u"))
-            nc.vector.quantize_mx(
-                out=w_cod[:, 256 * k:256 * (k + 1)].bitcast(FP8X4),
-                scales=w_scl[:, 256 * k:256 * (k + 1)],
-                in_=w_grp[:, 1024 * k:1024 * (k + 1)],
-            )
+        def w_quant(a):
+            for c0, n in ((0, 256), (256, 128)):
+                nc.vector.quantize_mx(
+                    out=w_cod[a][:, c0:c0 + n].bitcast(FP8X4),
+                    scales=w_scl[a][:, c0:c0 + n],
+                    in_=w_grp[a][:, 4 * c0:4 * (c0 + n)],
+                )
 
         x_cols = x_grp[:].rearrange("p (n j) -> p n j", j=4)
 
@@ -106,58 +110,76 @@ def tile_skeletonconv_kernel(tc, x, weight, dilation, step, out):
                 in_=x_grp[:, 4 * c0:4 * (c0 + n)],
             )
 
-        def x_move():
-            n = COLS - SHIFT
-            nc.vector.tensor_copy(out=x_cod[0][:, SHIFT:COLS].bitcast(I32), in_=x_cod[1][:, 0:n].bitcast(I32))
-            nc.vector.tensor_copy(out=x_scl[0][:, SHIFT:COLS].bitcast(I32), in_=x_scl[1][:, 0:n].bitcast(I32))
-            nc.vector.tensor_copy(out=x_cod[2][:, 0:n].bitcast(I32), in_=x_cod[1][:, SHIFT:COLS].bitcast(I32))
-            nc.vector.tensor_copy(out=x_scl[2][:, 0:n].bitcast(I32), in_=x_scl[1][:, SHIFT:COLS].bitcast(I32))
+        def x_move(lo, hi):
+            for t, d in ((0, -SHIFT), (2, SHIFT)):
+                a0 = max(lo, -d, 0)
+                a1 = min(hi, COLS - d, COLS)
+                for til in (x_cod, x_scl):
+                    nc.vector.tensor_copy(out=til[t][:, a0:a1].bitcast(I32), in_=til[1][:, a0 + d:a1 + d].bitcast(I32))
 
-        w_split(0)
+        def product(a, k, eng):
+            acc = psa.tile([P, 512], F32, name="acc")
+            for n0, n in ((0, 256), (256, 128)):
+                c0 = THIRD * k + n0
+                for i, t in enumerate((1, 0, 2)):
+                    nc.tensor.matmul_mx(
+                        out=acc[:, n0:n0 + n],
+                        lhsT=w_cod[a][:, P * t:P * (t + 1)].bitcast(FP8X4),
+                        lhsT_scale=w_scl[a][:, P * t:P * (t + 1)],
+                        rhs=x_cod[t][:, c0:c0 + n].bitcast(FP8X4),
+                        rhs_scale=x_scl[t][:, c0:c0 + n],
+                        start=(i == 0),
+                        stop=(i == 2),
+                    )
+            src = acc[:, k:k + RPT * PITCH].rearrange("p (r q) -> p r q", q=PITCH)[:, :, 0:W]
+            dst = res[a][:, RPT * k:RPT * (k + 1), :]
+            if eng == "v":
+                nc.vector.tensor_copy(out=dst, in_=src)
+            else:
+                nc.scalar.copy(out=dst, in_=src)
+            if k >= 1:
+                b = k - 1
+                nc.sync.dma_start(
+                    out=out[b, P * a:P * (a + 1)].rearrange("o h w -> o (h w)"),
+                    in_=res[a][:, 17 * b:17 * b + H, :].rearrange("p r w -> p (r w)"),
+                )
+
+        ctx.enter_context(tc.manual_schedule())
+        load_w(0)
+        load_x(0)
+        load_x(1)
+        load_w(1)
+        load_w(2)
+        load_w(3)
+        zeros()
+        w_split(0, "v")
+        w_turn(0)
         x_group(0)
         x_group(1)
+        w_split(1, "s")
+        w_turn(1)
         x_quant(0, 512)
+        w_quant(0)
         x_quant(512, 512)
         x_quant(1024, 128)
-        x_move()
-        w_pair(0)
-        w_split(1)
-        w_pair(1)
-        w_pair(2)
-        w_split(2)
-        w_pair(3)
-        w_split(3)
-        w_pair(4)
-        w_pair(5)
-
-        n_exit = 0
-        for a in range(NOT):
-            res = outs.tile([P, ROWS, W], F32, name="res")
-            for k in range(3):
-                acc = psa.tile([P, 512], F32, name="acc")
-                for n0, n in ((0, 256), (256, 128)):
-                    c0 = THIRD * k + n0
-                    for i, t in enumerate((1, 0, 2)):
-                        un = TAPS * a + t
-                        nc.tensor.matmul_mx(
-                            out=acc[:, n0:n0 + n],
-                            lhsT=w_cod[:, P * un:P * (un + 1)].bitcast(FP8X4),
-                            lhsT_scale=w_scl[:, P * un:P * (un + 1)],
-                            rhs=x_cod[t][:, c0:c0 + n].bitcast(FP8X4),
-                            rhs_scale=x_scl[t][:, c0:c0 + n],
-                            start=(i == 0),
-                            stop=(i == 2),
-                        )
-                src = acc[:, k:k + RPT * PITCH].rearrange("p (r q) -> p r q", q=PITCH)[:, :, 0:W]
-                dst = res[:, RPT * k:RPT * (k + 1), :]
-                if n_exit % 2 == 0:
-                    nc.vector.tensor_copy(out=dst, in_=src)
-                else:
-                    nc.scalar.copy(out=dst, in_=src)
-                n_exit += 1
-                if k >= 1:
-                    b = k - 1
-                    nc.sync.dma_start(
-                        out=out[b, P * a:P * (a + 1)].rearrange("o h w -> o (h w)"),
-                        in_=res[:, 17 * b:17 * b + H, :].rearrange("p r w -> p (r w)"),
-                    )
+        x_move(0, THIRD)
+        x_move(THIRD, COLS)
+        product(0, 0, "s")
+        product(0, 1, "s")
+        product(0, 2, "s")
+        w_quant(1)
+        w_split(2, "v")
+        product(1, 0, "s")
+        w_turn(2)
+        w_split(3, "v")
+        product(1, 1, "s")
+        product(1, 2, "s")
+        w_turn(3)
+        w_quant(2)
+        product(2, 0, "s")
+        product(2, 1, "s")
+        product(2, 2, "s")
+        w_quant(3)
+        product(3, 0, "s")
+        product(3, 1, "v")
+        product(3, 2, "s")

@@ -31,8 +31,8 @@ def tile_skeletonconv_kernel(tc, x, weight, dilation, step, out):
     assert dilation == 1 and step == 1
     with ExitStack() as ctx:
         keep = ctx.enter_context(tc.tile_pool(name="keep", bufs=1))
-        pst = ctx.enter_context(tc.psum_pool(name="pst", bufs=3))
-        psa = ctx.enter_context(tc.psum_pool(name="psa", bufs=5))
+        pst = ctx.enter_context(tc.psum_pool(name="pst", bufs=2))
+        psa = ctx.enter_context(tc.psum_pool(name="psa", bufs=6))
 
         ident = keep.tile([P, P], F32, name="ident")
         w_raw = [keep.tile([P, 1536], BF16, name="w_raw%d" % a) for a in range(NOT)]
@@ -110,39 +110,51 @@ def tile_skeletonconv_kernel(tc, x, weight, dilation, step, out):
                 in_=x_grp[:, 4 * c0:4 * (c0 + n)],
             )
 
-        def x_move(lo, hi):
-            for t, d in ((0, -SHIFT), (2, SHIFT)):
-                a0 = max(lo, -d, 0)
-                a1 = min(hi, COLS - d, COLS)
-                for til in (x_cod, x_scl):
-                    nc.vector.tensor_copy(out=til[t][:, a0:a1].bitcast(I32), in_=til[1][:, a0 + d:a1 + d].bitcast(I32))
+        def x_move(t):
+            d = SHIFT * (t - 1)
+            a0 = max(-d, 0)
+            a1 = min(COLS - d, COLS)
+            for til in (x_cod, x_scl):
+                nc.vector.tensor_copy(out=til[t][:, a0:a1].bitcast(I32), in_=til[1][:, a0 + d:a1 + d].bitcast(I32))
 
-        def product(a, k, eng):
-            acc = psa.tile([P, 512], F32, name="acc")
-            for n0, n in ((0, 256), (256, 128)):
-                c0 = THIRD * k + n0
+        accs = {}
+
+        def mx_pass(a, k, n0, n, i, t):
+            c0 = THIRD * k + n0
+            nc.tensor.matmul_mx(
+                out=accs[(a, k)][:, n0:n0 + n],
+                lhsT=w_cod[a][:, P * t:P * (t + 1)].bitcast(FP8X4),
+                lhsT_scale=w_scl[a][:, P * t:P * (t + 1)],
+                rhs=x_cod[t][:, c0:c0 + n].bitcast(FP8X4),
+                rhs_scale=x_scl[t][:, c0:c0 + n],
+                start=(i == 0),
+                stop=(i == 2),
+            )
+
+        def wide(a):
+            for k in range(3):
+                acc = psa.tile([P, 512], F32, name="acc")
+                accs[(a, k)] = acc
+            for i, t in enumerate((1, 0, 2)):
+                for k in range(3):
+                    mx_pass(a, k, 0, 256, i, t)
+
+        def narrow(a, engs):
+            for k in range(3):
                 for i, t in enumerate((1, 0, 2)):
-                    nc.tensor.matmul_mx(
-                        out=acc[:, n0:n0 + n],
-                        lhsT=w_cod[a][:, P * t:P * (t + 1)].bitcast(FP8X4),
-                        lhsT_scale=w_scl[a][:, P * t:P * (t + 1)],
-                        rhs=x_cod[t][:, c0:c0 + n].bitcast(FP8X4),
-                        rhs_scale=x_scl[t][:, c0:c0 + n],
-                        start=(i == 0),
-                        stop=(i == 2),
+                    mx_pass(a, k, 256, 128, i, t)
+                src = accs[(a, k)][:, k:k + RPT * PITCH].rearrange("p (r q) -> p r q", q=PITCH)[:, :, 0:W]
+                dst = res[a][:, RPT * k:RPT * (k + 1), :]
+                if engs[k] == "v":
+                    nc.vector.tensor_copy(out=dst, in_=src)
+                else:
+                    nc.scalar.copy(out=dst, in_=src)
+                if k >= 1:
+                    b = k - 1
+                    nc.sync.dma_start(
+                        out=out[b, P * a:P * (a + 1)].rearrange("o h w -> o (h w)"),
+                        in_=res[a][:, 17 * b:17 * b + H, :].rearrange("p r w -> p (r w)"),
                     )
-            src = acc[:, k:k + RPT * PITCH].rearrange("p (r q) -> p r q", q=PITCH)[:, :, 0:W]
-            dst = res[a][:, RPT * k:RPT * (k + 1), :]
-            if eng == "v":
-                nc.vector.tensor_copy(out=dst, in_=src)
-            else:
-                nc.scalar.copy(out=dst, in_=src)
-            if k >= 1:
-                b = k - 1
-                nc.sync.dma_start(
-                    out=out[b, P * a:P * (a + 1)].rearrange("o h w -> o (h w)"),
-                    in_=res[a][:, 17 * b:17 * b + H, :].rearrange("p r w -> p (r w)"),
-                )
 
         ctx.enter_context(tc.manual_schedule())
         load_w(0)
@@ -162,24 +174,20 @@ def tile_skeletonconv_kernel(tc, x, weight, dilation, step, out):
         w_quant(0)
         x_quant(512, 512)
         x_quant(1024, 128)
-        x_move(0, THIRD)
-        x_move(THIRD, COLS)
-        product(0, 0, "s")
-        product(0, 1, "s")
-        product(0, 2, "s")
+        x_move(0)
+        x_move(2)
+        wide(0)
+        narrow(0, "sss")
         w_quant(1)
         w_split(2, "v")
-        product(1, 0, "s")
-        w_turn(2)
         w_split(3, "v")
-        product(1, 1, "s")
-        product(1, 2, "s")
+        wide(1)
+        w_turn(2)
+        narrow(1, "sss")
         w_turn(3)
         w_quant(2)
-        product(2, 0, "s")
-        product(2, 1, "s")
-        product(2, 2, "s")
+        wide(2)
+        narrow(2, "sss")
         w_quant(3)
-        product(3, 0, "s")
-        product(3, 1, "v")
-        product(3, 2, "s")
+        wide(3)
+        narrow(3, "svs")

@@ -31,8 +31,8 @@ def tile_skeletonconv_kernel(tc, x, weight, dilation, step, out):
     assert dilation == 1 and step == 1
     with ExitStack() as ctx:
         keep = ctx.enter_context(tc.tile_pool(name="keep", bufs=1))
-        pst = ctx.enter_context(tc.psum_pool(name="pst", bufs=2))
-        psa = ctx.enter_context(tc.psum_pool(name="psa", bufs=6))
+        pst = ctx.enter_context(tc.psum_pool(name="pst", bufs=4))
+        psa = ctx.enter_context(tc.psum_pool(name="psa", bufs=4))
 
         ident = keep.tile([P, P], F32, name="ident")
         w_raw = [keep.tile([P, 1536], BF16, name="w_raw%d" % a) for a in range(NOT)]
@@ -110,51 +110,39 @@ def tile_skeletonconv_kernel(tc, x, weight, dilation, step, out):
                 in_=x_grp[:, 4 * c0:4 * (c0 + n)],
             )
 
-        def x_move(t):
-            d = SHIFT * (t - 1)
-            a0 = max(-d, 0)
-            a1 = min(COLS - d, COLS)
-            for til in (x_cod, x_scl):
-                nc.vector.tensor_copy(out=til[t][:, a0:a1].bitcast(I32), in_=til[1][:, a0 + d:a1 + d].bitcast(I32))
+        def x_move(lo, hi):
+            for t, d in ((0, -SHIFT), (2, SHIFT)):
+                a0 = max(lo, -d, 0)
+                a1 = min(hi, COLS - d, COLS)
+                for til in (x_cod, x_scl):
+                    nc.vector.tensor_copy(out=til[t][:, a0:a1].bitcast(I32), in_=til[1][:, a0 + d:a1 + d].bitcast(I32))
 
-        accs = {}
-
-        def mx_pass(a, k, n0, n, i, t):
-            c0 = THIRD * k + n0
-            nc.tensor.matmul_mx(
-                out=accs[(a, k)][:, n0:n0 + n],
-                lhsT=w_cod[a][:, P * t:P * (t + 1)].bitcast(FP8X4),
-                lhsT_scale=w_scl[a][:, P * t:P * (t + 1)],
-                rhs=x_cod[t][:, c0:c0 + n].bitcast(FP8X4),
-                rhs_scale=x_scl[t][:, c0:c0 + n],
-                start=(i == 0),
-                stop=(i == 2),
-            )
-
-        def wide(a):
-            for k in range(3):
-                acc = psa.tile([P, 512], F32, name="acc")
-                accs[(a, k)] = acc
-            for i, t in enumerate((1, 0, 2)):
-                for k in range(3):
-                    mx_pass(a, k, 0, 256, i, t)
-
-        def narrow(a, engs):
-            for k in range(3):
+        def product(a, k, eng):
+            acc = psa.tile([P, 512], F32, name="acc")
+            for n0, n in ((0, 256), (256, 128)):
+                c0 = THIRD * k + n0
                 for i, t in enumerate((1, 0, 2)):
-                    mx_pass(a, k, 256, 128, i, t)
-                src = accs[(a, k)][:, k:k + RPT * PITCH].rearrange("p (r q) -> p r q", q=PITCH)[:, :, 0:W]
-                dst = res[a][:, RPT * k:RPT * (k + 1), :]
-                if engs[k] == "v":
-                    nc.vector.tensor_copy(out=dst, in_=src)
-                else:
-                    nc.scalar.copy(out=dst, in_=src)
-                if k >= 1:
-                    b = k - 1
-                    nc.sync.dma_start(
-                        out=out[b, P * a:P * (a + 1)].rearrange("o h w -> o (h w)"),
-                        in_=res[a][:, 17 * b:17 * b + H, :].rearrange("p r w -> p (r w)"),
+                    nc.tensor.matmul_mx(
+                        out=acc[:, n0:n0 + n],
+                        lhsT=w_cod[a][:, P * t:P * (t + 1)].bitcast(FP8X4),
+                        lhsT_scale=w_scl[a][:, P * t:P * (t + 1)],
+                        rhs=x_cod[t][:, c0:c0 + n].bitcast(FP8X4),
+                        rhs_scale=x_scl[t][:, c0:c0 + n],
+                        start=(i == 0),
+                        stop=(i == 2),
                     )
+            src = acc[:, k:k + RPT * PITCH].rearrange("p (r q) -> p r q", q=PITCH)[:, :, 0:W]
+            dst = res[a][:, RPT * k:RPT * (k + 1), :]
+            if eng == "v":
+                nc.vector.tensor_copy(out=dst, in_=src)
+            else:
+                nc.scalar.copy(out=dst, in_=src)
+            if k >= 1:
+                b = k - 1
+                nc.sync.dma_start(
+                    out=out[b, P * a:P * (a + 1)].rearrange("o h w -> o (h w)"),
+                    in_=res[a][:, 17 * b:17 * b + H, :].rearrange("p r w -> p (r w)"),
+                )
 
         ctx.enter_context(tc.manual_schedule())
         load_w(0)
@@ -169,25 +157,30 @@ def tile_skeletonconv_kernel(tc, x, weight, dilation, step, out):
         x_group(0)
         x_group(1)
         w_split(1, "s")
+        w_split(2, "s")
         w_turn(1)
         x_quant(0, 512)
         w_quant(0)
         x_quant(512, 512)
         x_quant(1024, 128)
-        x_move(0)
-        x_move(2)
-        wide(0)
-        narrow(0, "sss")
+        x_move(0, THIRD)
+        x_move(THIRD, 2 * THIRD)
+        x_move(2 * THIRD, COLS)
+        product(0, 0, "s")
+        product(0, 1, "s")
+        product(0, 2, "s")
         w_quant(1)
-        w_split(2, "v")
         w_split(3, "v")
-        wide(1)
         w_turn(2)
-        narrow(1, "sss")
         w_turn(3)
         w_quant(2)
-        wide(2)
-        narrow(2, "sss")
+        product(1, 0, "s")
+        product(1, 1, "s")
+        product(1, 2, "s")
         w_quant(3)
-        wide(3)
-        narrow(3, "svs")
+        product(2, 0, "v")
+        product(2, 1, "s")
+        product(2, 2, "v")
+        product(3, 0, "s")
+        product(3, 1, "v")
+        product(3, 2, "s")

@@ -31,8 +31,8 @@ def tile_skeletonconv_kernel(tc, x, weight, dilation, step, out):
     assert dilation == 1 and step == 1
     with ExitStack() as ctx:
         keep = ctx.enter_context(tc.tile_pool(name="keep", bufs=1))
-        pst = ctx.enter_context(tc.psum_pool(name="pst", bufs=4))
-        psa = ctx.enter_context(tc.psum_pool(name="psa", bufs=4))
+        pst = ctx.enter_context(tc.psum_pool(name="pst", bufs=3))
+        psa = ctx.enter_context(tc.psum_pool(name="psa", bufs=5))
 
         ident = keep.tile([P, P], F32, name="ident")
         w_raw = [keep.tile([P, 1536], BF16, name="w_raw%d" % a) for a in range(NOT)]
@@ -44,6 +44,7 @@ def tile_skeletonconv_kernel(tc, x, weight, dilation, step, out):
         x_grp = keep.tile([P, 1160 * 4], BF16, name="x_grp", align_bytes=64)
         x_cod = [keep.tile([P, COLS], U32, name="x_cod%d" % t, align_bytes=64) for t in range(TAPS)]
         x_scl = [keep.tile([P, COLS], U8, name="x_scl%d" % t, align_bytes=64) for t in range(TAPS)]
+        idle_in = keep.tile([P, 512], BF16, name="idle_in")
         res = [keep.tile([P, ROWS, W], F32, name="res%d" % a) for a in range(NOT)]
 
         w_view = weight.rearrange("(a p) c t -> a p (c t)", p=P)
@@ -65,6 +66,12 @@ def tile_skeletonconv_kernel(tc, x, weight, dilation, step, out):
             nc.vector.memset(x_cod[2][:, COLS - SHIFT:COLS].bitcast(I32), 0)
             nc.vector.memset(x_scl[0][:, 0:SHIFT].bitcast(I32), 0)
             nc.vector.memset(x_scl[2][:, COLS - SHIFT:COLS].bitcast(I32), 0)
+
+        def warm_up():
+            nc.gpsimd.memset(idle_in[:], 0.0)
+            idle_out = psa.tile([P, 512], F32, name="acc")
+            for i in range(8):
+                nc.tensor.matmul(idle_out[:], lhsT=idle_in[:, 0:P], rhs=idle_in[:], start=True, stop=True)
 
         def w_split(a, eng):
             dst = w_tap[a][:].rearrange("p (t c) -> p t c", t=TAPS)
@@ -154,33 +161,33 @@ def tile_skeletonconv_kernel(tc, x, weight, dilation, step, out):
         zeros()
         w_split(0, "v")
         w_turn(0)
+        warm_up()
         x_group(0)
         x_group(1)
         w_split(1, "s")
-        w_split(2, "s")
         w_turn(1)
         x_quant(0, 512)
         w_quant(0)
         x_quant(512, 512)
         x_quant(1024, 128)
         x_move(0, THIRD)
-        x_move(THIRD, 2 * THIRD)
-        x_move(2 * THIRD, COLS)
+        x_move(THIRD, COLS)
         product(0, 0, "s")
         product(0, 1, "s")
         product(0, 2, "s")
         w_quant(1)
-        w_split(3, "v")
-        w_turn(2)
-        w_turn(3)
-        w_quant(2)
+        w_split(2, "v")
         product(1, 0, "s")
+        w_turn(2)
+        w_split(3, "v")
         product(1, 1, "s")
         product(1, 2, "s")
-        w_quant(3)
-        product(2, 0, "v")
+        w_turn(3)
+        w_quant(2)
+        product(2, 0, "s")
         product(2, 1, "s")
-        product(2, 2, "v")
+        product(2, 2, "s")
+        w_quant(3)
         product(3, 0, "s")
         product(3, 1, "v")
         product(3, 2, "s")

@@ -70,7 +70,7 @@ def tile_skeletonconv_kernel(tc, x, weight, dilation, step, out):
         def warm_up():
             nc.gpsimd.memset(idle_in[:], 0.0)
             idle_out = psa.tile([P, 512], F32, name="acc")
-            for i in range(8):
+            for i in range(5):
                 nc.tensor.matmul(idle_out[:], lhsT=idle_in[:, 0:P], rhs=idle_in[:], start=True, stop=True)
 
         def w_split(a, eng):

@@ -70,16 +70,17 @@ def tile_skeletonconv_kernel(tc, x, weight, dilation, step, out):
         def warm_up():
             nc.gpsimd.memset(idle_in[:], 0.0)
             idle_out = psa.tile([P, 512], F32, name="acc")
-            for i in range(5):
+            for i in range(8):
                 nc.tensor.matmul(idle_out[:], lhsT=idle_in[:, 0:P], rhs=idle_in[:], start=True, stop=True)
 
         def w_split(a, eng):
             dst = w_tap[a][:].rearrange("p (t c) -> p t c", t=TAPS)
             src = w_raw[a][:].rearrange("p (c t) -> p t c", t=TAPS)
-            if eng == "v":
-                nc.vector.tensor_copy(out=dst, in_=src)
-            else:
-                nc.scalar.copy(out=dst, in_=src)
+            for t in range(TAPS):
+                if eng == "v":
+                    nc.vector.tensor_copy(out=dst[:, t, :], in_=src[:, t, :])
+                else:
+                    nc.scalar.copy(out=dst[:, t, :], in_=src[:, t, :])
 
         def w_turn(a):
             words = w_tap[a][:].bitcast(F32)

@@ -18,12 +18,11 @@ H = 16
 W = 32
 TAPS = 3
 NOT = 4
-PITCH = 35
-ROWS = 33
-COLS = 1152
-SHIFT = PITCH + 1
-THIRD = 384
-RPT = 11
+PITCH = 33
+COLS = 1216
+OFF = 32
+BASE = (17, 608)
+WINDOWS = ((0, 512), (512, 128), (640, 512))
 
 
 def tile_skeletonconv_kernel(tc, x, weight, dilation, step, out):
@@ -41,11 +40,11 @@ def tile_skeletonconv_kernel(tc, x, weight, dilation, step, out):
         w_cod = [keep.tile([P, TAPS * P], U32, name="w_cod%d" % a, align_bytes=64) for a in range(NOT)]
         w_scl = [keep.tile([P, TAPS * P], U8, name="w_scl%d" % a, align_bytes=64) for a in range(NOT)]
         x_raw = [keep.tile([P, 4, 512], BF16, name="x_raw%d" % b) for b in range(NB)]
-        x_grp = keep.tile([P, 1160 * 4], BF16, name="x_grp", align_bytes=64)
-        x_cod = [keep.tile([P, COLS], U32, name="x_cod%d" % t, align_bytes=64) for t in range(TAPS)]
-        x_scl = [keep.tile([P, COLS], U8, name="x_scl%d" % t, align_bytes=64) for t in range(TAPS)]
+        x_grp = keep.tile([P, COLS * 4], BF16, name="x_grp", align_bytes=64)
+        x_cod = keep.tile([P, COLS], U32, name="x_cod", align_bytes=64)
+        x_scl = [keep.tile([P, COLS], U8, name="x_scl%d" % s, align_bytes=64) for s in range(2)]
         idle_in = keep.tile([P, 512], BF16, name="idle_in")
-        res = [keep.tile([P, ROWS, W], F32, name="res%d" % a) for a in range(NOT)]
+        res = [keep.tile([P, NB * H, W], F32, name="res%d" % a) for a in range(NOT)]
 
         w_view = weight.rearrange("(a p) c t -> a p (c t)", p=P)
 
@@ -61,11 +60,7 @@ def tile_skeletonconv_kernel(tc, x, weight, dilation, step, out):
         def zeros():
             make_identity(nc, ident[:])
             nc.vector.memset(x_grp[:].bitcast(I32), 0)
-            nc.vector.memset(x_scl[1][:].bitcast(I32), 0)
-            nc.vector.memset(x_cod[0][:, 0:SHIFT].bitcast(I32), 0)
-            nc.vector.memset(x_cod[2][:, COLS - SHIFT:COLS].bitcast(I32), 0)
-            nc.vector.memset(x_scl[0][:, 0:SHIFT].bitcast(I32), 0)
-            nc.vector.memset(x_scl[2][:, COLS - SHIFT:COLS].bitcast(I32), 0)
+            nc.vector.memset(x_scl[0][:].bitcast(I32), 0)
 
         def warm_up():
             nc.gpsimd.memset(idle_in[:], 0.0)
@@ -104,43 +99,50 @@ def tile_skeletonconv_kernel(tc, x, weight, dilation, step, out):
         x_cols = x_grp[:].rearrange("p (n j) -> p n j", j=4)
 
         def x_group(b):
-            base = 17 * PITCH * b
+            base = OFF + BASE[b]
             dst = x_cols[:, base:base + H * PITCH, :].rearrange("p (h q) j -> p h q j", q=PITCH)[:, :, 0:W, :]
             nc.vector.tensor_copy(
                 out=dst.rearrange("p h (c i) j -> p h c j i", i=4),
-                in_=x_raw[b][:].rearrange("p j (h c i) -> p h c j i", h=H, i=4),
+                in_=x_raw[b][:].rearrange("p j (h c i) -> p h c j i", h=H, i=4)[:, ::-1, :, :, :],
             )
 
         def x_quant(c0, n):
             nc.vector.quantize_mx(
-                out=x_cod[1][:, c0:c0 + n].bitcast(FP8X4),
-                scales=x_scl[1][:, c0:c0 + n],
+                out=x_cod[:, c0:c0 + n].bitcast(FP8X4),
+                scales=x_scl[0][:, c0:c0 + n],
                 in_=x_grp[:, 4 * c0:4 * (c0 + n)],
             )
 
-        def x_move(lo, hi):
-            for t, d in ((0, -SHIFT), (2, SHIFT)):
-                a0 = max(lo, -d, 0)
-                a1 = min(hi, COLS - d, COLS)
-                for til in (x_cod, x_scl):
-                    nc.vector.tensor_copy(out=til[t][:, a0:a1].bitcast(I32), in_=til[1][:, a0 + d:a1 + d].bitcast(I32))
+        def x_plane(lo, hi):
+            nc.vector.tensor_copy(out=x_scl[1][:, lo:hi].bitcast(I32), in_=x_scl[0][:, lo + 32:hi + 32].bitcast(I32))
 
         def product(a, k, eng):
+            g0, n = WINDOWS[k]
             acc = psa.tile([P, 512], F32, name="acc")
-            for n0, n in ((0, 256), (256, 128)):
-                c0 = THIRD * k + n0
-                for i, t in enumerate((1, 0, 2)):
-                    nc.tensor.matmul_mx(
-                        out=acc[:, n0:n0 + n],
-                        lhsT=w_cod[a][:, P * t:P * (t + 1)].bitcast(FP8X4),
-                        lhsT_scale=w_scl[a][:, P * t:P * (t + 1)],
-                        rhs=x_cod[t][:, c0:c0 + n].bitcast(FP8X4),
-                        rhs_scale=x_scl[t][:, c0:c0 + n],
-                        start=(i == 0),
-                        stop=(i == 2),
-                    )
-            src = acc[:, k:k + RPT * PITCH].rearrange("p (r q) -> p r q", q=PITCH)[:, :, 0:W]
-            dst = res[a][:, RPT * k:RPT * (k + 1), :]
+            for i, t in enumerate((1, 0, 2)):
+                c0 = g0 + OFF + 32 - 32 * t
+                if t == 1:
+                    plane = x_scl[1][:, g0:g0 + n]
+                else:
+                    plane = x_scl[0][:, c0:c0 + n]
+                nc.tensor.matmul_mx(
+                    out=acc[:, 0:n],
+                    lhsT=w_cod[a][:, P * t:P * (t + 1)].bitcast(FP8X4),
+                    lhsT_scale=w_scl[a][:, P * t:P * (t + 1)],
+                    rhs=x_cod[:, c0:c0 + n].bitcast(FP8X4),
+                    rhs_scale=plane,
+                    start=(i == 0),
+                    stop=(i == 2),
+                )
+            if k == 0:
+                src = acc[:, 17:512].rearrange("p (r q) -> p r q", q=PITCH)[:, ::-1, 0:W]
+                dst = res[a][:, 1:H, :]
+            elif k == 1:
+                src = acc[:, 0:128].rearrange("p (r q) -> p r q", q=W)[:, 0:4:3, :]
+                dst = res[a][:, 0:2 * H:2 * H - 1, :]
+            else:
+                src = acc[:, 1:496].rearrange("p (r q) -> p r q", q=PITCH)[:, ::-1, 0:W]
+                dst = res[a][:, H:2 * H - 1, :]
             if eng == "v":
                 nc.vector.tensor_copy(out=dst, in_=src)
             else:
@@ -149,7 +151,7 @@ def tile_skeletonconv_kernel(tc, x, weight, dilation, step, out):
                 b = k - 1
                 nc.sync.dma_start(
                     out=out[b, P * a:P * (a + 1)].rearrange("o h w -> o (h w)"),
-                    in_=res[a][:, 17 * b:17 * b + H, :].rearrange("p r w -> p (r w)"),
+                    in_=res[a][:, H * b:H * (b + 1), :].rearrange("p r w -> p (r w)"),
                 )
 
         ctx.enter_context(tc.manual_schedule())
@@ -170,9 +172,10 @@ def tile_skeletonconv_kernel(tc, x, weight, dilation, step, out):
         x_quant(0, 512)
         w_quant(0)
         x_quant(512, 512)
+        x_plane(0, 512)
         x_quant(1024, 128)
-        x_move(0, THIRD)
-        x_move(THIRD, COLS)
+        x_quant(1152, 64)
+        x_plane(512, 1152)
         product(0, 0, "s")
         product(0, 1, "s")
         product(0, 2, "s")

@@ -30,8 +30,8 @@ def tile_skeletonconv_kernel(tc, x, weight, dilation, step, out):
     assert dilation == 1 and step == 1
     with ExitStack() as ctx:
         keep = ctx.enter_context(tc.tile_pool(name="keep", bufs=1))
-        pst = ctx.enter_context(tc.psum_pool(name="pst", bufs=3))
-        psa = ctx.enter_context(tc.psum_pool(name="psa", bufs=5))
+        pst = ctx.enter_context(tc.psum_pool(name="pst", bufs=4))
+        psa = ctx.enter_context(tc.psum_pool(name="psa", bufs=4))
 
         ident = keep.tile([P, P], F32, name="ident")
         w_raw = [keep.tile([P, 1536], BF16, name="w_raw%d" % a) for a in range(NOT)]
@@ -59,13 +59,21 @@ def tile_skeletonconv_kernel(tc, x, weight, dilation, step, out):
 
         def zeros():
             make_identity(nc, ident[:])
-            nc.vector.memset(x_grp[:].bitcast(I32), 0)
-            nc.vector.memset(x_scl[0][:].bitcast(I32), 0)
-
-        def warm_up():
+            words = x_grp[:].bitcast(I32)
+            for b in range(NB):
+                c0 = OFF + BASE[b]
+                lo = (0, c0 - 64)[b]
+                nc.vector.memset(words[:, 2 * lo:2 * c0], 0)
+                pad = words[:, 2 * (c0 + W):2 * (c0 + W + (H - 1) * PITCH)].rearrange("p (r q) -> p r q", q=2 * PITCH)
+                nc.vector.memset(pad[:, :, 0:2], 0)
+            nc.vector.memset(words[:, 2 * (OFF + BASE[1] + H * PITCH - 1):2 * COLS], 0)
+            nc.gpsimd.memset(x_scl[0][:].bitcast(F32), 0.0)
             nc.gpsimd.memset(idle_in[:], 0.0)
-            idle_out = psa.tile([P, 512], F32, name="acc")
-            for i in range(8):
+
+        idle_out = psa.tile([P, 512], F32, name="acc")
+
+        def warm_up(n):
+            for i in range(n):
                 nc.tensor.matmul(idle_out[:], lhsT=idle_in[:, 0:P], rhs=idle_in[:], start=True, stop=True)
 
         def w_split(a, eng):
@@ -119,7 +127,7 @@ def tile_skeletonconv_kernel(tc, x, weight, dilation, step, out):
         def product(a, k, eng):
             g0, n = WINDOWS[k]
             acc = psa.tile([P, 512], F32, name="acc")
-            for i, t in enumerate((1, 0, 2)):
+            for i, t in enumerate((2, 0, 1)):
                 c0 = g0 + OFF + 32 - 32 * t
                 if t == 1:
                     plane = x_scl[1][:, g0:g0 + n]
@@ -157,41 +165,42 @@ def tile_skeletonconv_kernel(tc, x, weight, dilation, step, out):
         ctx.enter_context(tc.manual_schedule())
         load_w(0)
         load_x(0)
-        load_x(1)
         load_w(1)
         load_w(2)
         load_w(3)
+        load_x(1)
         zeros()
+        x_quant(576, 64)
         w_split(0, "v")
         w_turn(0)
-        warm_up()
+        warm_up(4)
         x_group(0)
-        x_group(1)
         w_split(1, "s")
-        w_turn(1)
-        x_quant(0, 512)
         w_quant(0)
-        x_quant(512, 512)
+        x_quant(0, 512)
+        x_quant(512, 64)
         x_plane(0, 512)
-        x_quant(1024, 128)
-        x_quant(1152, 64)
-        x_plane(512, 1152)
         product(0, 0, "s")
-        product(0, 1, "s")
-        product(0, 2, "s")
-        w_quant(1)
+        w_turn(1)
         w_split(2, "v")
-        product(1, 0, "s")
         w_turn(2)
         w_split(3, "v")
-        product(1, 1, "s")
-        product(1, 2, "s")
         w_turn(3)
+        x_group(1)
+        w_quant(1)
+        product(1, 0, "s")
+        x_quant(640, 512)
+        x_quant(1152, 64)
+        x_plane(512, 1152)
         w_quant(2)
-        product(2, 0, "s")
-        product(2, 1, "s")
-        product(2, 2, "s")
         w_quant(3)
-        product(3, 0, "s")
+        product(0, 1, "v")
+        product(0, 2, "v")
+        product(1, 1, "v")
+        product(1, 2, "s")
+        product(2, 0, "v")
+        product(2, 1, "v")
+        product(2, 2, "s")
+        product(3, 0, "v")
         product(3, 1, "v")
         product(3, 2, "s")

@@ -184,8 +184,10 @@ def tile_skeletonconv_kernel(tc, x, weight, dilation, step, out):
         w_turn(1)
         w_split(2, "v")
         w_turn(2)
+        warm_up(2)
         w_split(3, "v")
         w_turn(3)
+        warm_up(3)
         x_group(1)
         w_quant(1)
         product(1, 0, "s")

@@ -162,6 +162,46 @@ def tile_skeletonconv_kernel(tc, x, weight, dilation, step, out):
                     in_=res[a][:, H * b:H * (b + 1), :].rearrange("p r w -> p (r w)"),
                 )
 
+        def last_product(a):
+            g0 = WINDOWS[2][0]
+            half = [psa.tile([P, 512], F32, name="acc") for s in range(2)]
+            for s in range(2):
+                for i, t in enumerate((2, 0, 1)):
+                    c0 = g0 + 256 * s + OFF + 32 - 32 * t
+                    if t == 1:
+                        plane = x_scl[1][:, g0 + 256 * s:g0 + 256 * (s + 1)]
+                    else:
+                        plane = x_scl[0][:, c0:c0 + 256]
+                    nc.tensor.matmul_mx(
+                        out=half[s][:, 0:256],
+                        lhsT=w_cod[a][:, P * t:P * (t + 1)].bitcast(FP8X4),
+                        lhsT_scale=w_scl[a][:, P * t:P * (t + 1)],
+                        rhs=x_cod[:, c0:c0 + 256].bitcast(FP8X4),
+                        rhs_scale=plane,
+                        start=(i == 0),
+                        stop=(i == 2),
+                    )
+                if s == 0:
+                    nc.vector.tensor_copy(
+                        out=res[a][:, H + 8:H + 15, :],
+                        in_=half[0][:, 1:1 + 7 * PITCH].rearrange("p (r q) -> p r q", q=PITCH)[:, ::-1, 0:W],
+                    )
+                    nc.sync.dma_start(
+                        out=out[1, P * a:P * (a + 1), 8:16, :].rearrange("o h w -> o (h w)"),
+                        in_=res[a][:, H + 8:H + 16, :].rearrange("p r w -> p (r w)"),
+                    )
+                    nc.vector.tensor_copy(out=res[a][:, H + 7, 0:24], in_=half[0][:, 232:256])
+                else:
+                    nc.scalar.copy(out=res[a][:, H + 7, 24:W], in_=half[1][:, 0:8])
+                    nc.scalar.copy(
+                        out=res[a][:, H:H + 7, :],
+                        in_=half[1][:, 9:9 + 7 * PITCH].rearrange("p (r q) -> p r q", q=PITCH)[:, ::-1, 0:W],
+                    )
+                    nc.sync.dma_start(
+                        out=out[1, P * a:P * (a + 1), 0:8, :].rearrange("o h w -> o (h w)"),
+                        in_=res[a][:, H:H + 8, :].rearrange("p r w -> p (r w)"),
+                    )
+
         ctx.enter_context(tc.manual_schedule())
         load_w(0)
         load_x(0)
@@ -205,4 +245,4 @@ def tile_skeletonconv_kernel(tc, x, weight, dilation, step, out):
         product(2, 2, "s")
         product(3, 0, "v")
         product(3, 1, "v")
-        product(3, 2, "s")
+        last_product(3)

from contextlib import ExitStack

import concourse.mybir as mybir
from concourse.masks import make_identity

FLOPS = 2 * 2 * 512 * 512 * 3 * 512

BF16 = mybir.dt.bfloat16
F32 = mybir.dt.float32
I32 = mybir.dt.int32
U32 = mybir.dt.uint32
U8 = mybir.dt.uint8
FP8X4 = mybir.dt.float8_e4m3fn_x4

P = 128
NB = 2
H = 16
W = 32
TAPS = 3
NOT = 4
PITCH = 33
COLS = 1216
OFF = 32
BASE = (17, 608)
WINDOWS = ((0, 512), (512, 128), (640, 512))


def tile_skeletonconv_kernel(tc, x, weight, dilation, step, out):
    nc = tc.nc
    assert dilation == 1 and step == 1
    with ExitStack() as ctx:
        keep = ctx.enter_context(tc.tile_pool(name="keep", bufs=1))
        pst = ctx.enter_context(tc.psum_pool(name="pst", bufs=4))
        psa = ctx.enter_context(tc.psum_pool(name="psa", bufs=4))

        ident = keep.tile([P, P], F32, name="ident")
        w_raw = [keep.tile([P, 1536], BF16, name="w_raw%d" % a) for a in range(NOT)]
        w_tap = [keep.tile([P, 1536], BF16, name="w_tap%d" % a) for a in range(NOT)]
        w_grp = [keep.tile([P, 1536], BF16, name="w_grp%d" % a, align_bytes=64) for a in range(NOT)]
        w_cod = [keep.tile([P, TAPS * P], U32, name="w_cod%d" % a, align_bytes=64) for a in range(NOT)]
        w_scl = [keep.tile([P, TAPS * P], U8, name="w_scl%d" % a, align_bytes=64) for a in range(NOT)]
        x_raw = [keep.tile([P, 4, 512], BF16, name="x_raw%d" % b) for b in range(NB)]
        x_grp = keep.tile([P, COLS * 4], BF16, name="x_grp", align_bytes=64)
        x_cod = keep.tile([P, COLS], U32, name="x_cod", align_bytes=64)
        x_scl = [keep.tile([P, COLS], U8, name="x_scl%d" % s, align_bytes=64) for s in range(2)]
        idle_in = keep.tile([P, 512], BF16, name="idle_in")
        res = [keep.tile([P, NB * H, W], F32, name="res%d" % a) for a in range(NOT)]

        w_view = weight.rearrange("(a p) c t -> a p (c t)", p=P)

        def load_w(a):
            nc.sync.dma_start(out=w_raw[a][:], in_=w_view[a])

        def load_x(b):
            nc.sync.dma_start(
                out=x_raw[b][:].rearrange("p (u e) n -> p u (e n)", u=2),
                in_=x[b].rearrange("(u p e) h w -> p u (e h w)", u=2, p=P, e=2),
            )

        def zeros():
            make_identity(nc, ident[:])
            words = x_grp[:].bitcast(I32)
            for b in range(NB):
                c0 = OFF + BASE[b]
                lo = (0, c0 - 64)[b]
                nc.vector.memset(words[:, 2 * lo:2 * c0], 0)
                pad = words[:, 2 * (c0 + W):2 * (c0 + W + (H - 1) * PITCH)].rearrange("p (r q) -> p r q", q=2 * PITCH)
                nc.vector.memset(pad[:, :, 0:2], 0)
            nc.vector.memset(words[:, 2 * (OFF + BASE[1] + H * PITCH - 1):2 * COLS], 0)
            nc.gpsimd.memset(x_scl[0][:].bitcast(F32), 0.0)
            nc.gpsimd.memset(idle_in[:], 0.0)

        idle_out = psa.tile([P, 512], F32, name="acc")

        def warm_up(n):
            for i in range(n):
                nc.tensor.matmul(idle_out[:], lhsT=idle_in[:, 0:P], rhs=idle_in[:], start=True, stop=True)

        def w_split(a, eng):
            dst = w_tap[a][:].rearrange("p (t c) -> p t c", t=TAPS)
            src = w_raw[a][:].rearrange("p (c t) -> p t c", t=TAPS)
            for t in range(TAPS):
                if eng == "v":
                    nc.vector.tensor_copy(out=dst[:, t, :], in_=src[:, t, :])
                else:
                    nc.scalar.copy(out=dst[:, t, :], in_=src[:, t, :])

        def w_turn(a):
            words = w_tap[a][:].bitcast(F32)
            grp32 = w_grp[a][:].bitcast(F32).rearrange("p (t o u) -> p t o u", t=TAPS, u=2)
            for t0, nt in ((0, 2), (2, 1)):
                pt = pst.tile([P, 2, 2, P], F32, name="pt")
                for i in range(nt):
                    for u in range(2):
                        c0 = 256 * (t0 + i) + P * u
                        nc.tensor.transpose(pt[:, i, u, :], words[:, c0:c0 + P], ident[:])
                nc.scalar.copy(out=grp32[:, t0:t0 + nt, :, :], in_=pt[:, 0:nt, :, :].rearrange("p i u o -> p i o u"))

        def w_quant(a):
            for c0, n in ((0, 256), (256, 128)):
                nc.vector.quantize_mx(
                    out=w_cod[a][:, c0:c0 + n].bitcast(FP8X4),
                    scales=w_scl[a][:, c0:c0 + n],
                    in_=w_grp[a][:, 4 * c0:4 * (c0 + n)],
                )

        x_cols = x_grp[:].rearrange("p (n j) -> p n j", j=4)

        def x_group(b):
            base = OFF + BASE[b]
            dst = x_cols[:, base:base + H * PITCH, :].rearrange("p (h q) j -> p h q j", q=PITCH)[:, :, 0:W, :]
            nc.vector.tensor_copy(
                out=dst.rearrange("p h (c i) j -> p h c j i", i=4),
                in_=x_raw[b][:].rearrange("p j (h c i) -> p h c j i", h=H, i=4)[:, ::-1, :, :, :],
            )

        def x_quant(c0, n):
            nc.vector.quantize_mx(
                out=x_cod[:, c0:c0 + n].bitcast(FP8X4),
                scales=x_scl[0][:, c0:c0 + n],
                in_=x_grp[:, 4 * c0:4 * (c0 + n)],
            )

        def x_plane(lo, hi):
            nc.vector.tensor_copy(out=x_scl[1][:, lo:hi].bitcast(I32), in_=x_scl[0][:, lo + 32:hi + 32].bitcast(I32))

        def product(a, k, eng):
            g0, n = WINDOWS[k]
            acc = psa.tile([P, 512], F32, name="acc")
            for i, t in enumerate((2, 0, 1)):
                c0 = g0 + OFF + 32 - 32 * t
                if t == 1:
                    plane = x_scl[1][:, g0:g0 + n]
                else:
                    plane = x_scl[0][:, c0:c0 + n]
                nc.tensor.matmul_mx(
                    out=acc[:, 0:n],
                    lhsT=w_cod[a][:, P * t:P * (t + 1)].bitcast(FP8X4),
                    lhsT_scale=w_scl[a][:, P * t:P * (t + 1)],
                    rhs=x_cod[:, c0:c0 + n].bitcast(FP8X4),
                    rhs_scale=plane,
                    start=(i == 0),
                    stop=(i == 2),
                )
            if k == 0:
                src = acc[:, 17:512].rearrange("p (r q) -> p r q", q=PITCH)[:, ::-1, 0:W]
                dst = res[a][:, 1:H, :]
            elif k == 1:
                src = acc[:, 0:128].rearrange("p (r q) -> p r q", q=W)[:, 0:4:3, :]
                dst = res[a][:, 0:2 * H:2 * H - 1, :]
            else:
                src = acc[:, 1:496].rearrange("p (r q) -> p r q", q=PITCH)[:, ::-1, 0:W]
                dst = res[a][:, H:2 * H - 1, :]
            if eng == "v":
                nc.vector.tensor_copy(out=dst, in_=src)
            else:
                nc.scalar.copy(out=dst, in_=src)
            if k >= 1:
                b = k - 1
                nc.sync.dma_start(
                    out=out[b, P * a:P * (a + 1)].rearrange("o h w -> o (h w)"),
                    in_=res[a][:, H * b:H * (b + 1), :].rearrange("p r w -> p (r w)"),
                )

        def last_product(a):
            g0 = WINDOWS[2][0]
            half = [psa.tile([P, 512], F32, name="acc") for s in range(2)]
            for s in range(2):
                for i, t in enumerate((2, 0, 1)):
                    c0 = g0 + 256 * s + OFF + 32 - 32 * t
                    if t == 1:
                        plane = x_scl[1][:, g0 + 256 * s:g0 + 256 * (s + 1)]
                    else:
                        plane = x_scl[0][:, c0:c0 + 256]
                    nc.tensor.matmul_mx(
                        out=half[s][:, 0:256],
                        lhsT=w_cod[a][:, P * t:P * (t + 1)].bitcast(FP8X4),
                        lhsT_scale=w_scl[a][:, P * t:P * (t + 1)],
                        rhs=x_cod[:, c0:c0 + 256].bitcast(FP8X4),
                        rhs_scale=plane,
                        start=(i == 0),
                        stop=(i == 2),
                    )
                if s == 0:
                    nc.vector.tensor_copy(
                        out=res[a][:, H + 8:H + 15, :],
                        in_=half[0][:, 1:1 + 7 * PITCH].rearrange("p (r q) -> p r q", q=PITCH)[:, ::-1, 0:W],
                    )
                    nc.sync.dma_start(
                        out=out[1, P * a:P * (a + 1), 8:16, :].rearrange("o h w -> o (h w)"),
                        in_=res[a][:, H + 8:H + 16, :].rearrange("p r w -> p (r w)"),
                    )
                    nc.vector.tensor_copy(out=res[a][:, H + 7, 0:24], in_=half[0][:, 232:256])
                else:
                    nc.scalar.copy(out=res[a][:, H + 7, 24:W], in_=half[1][:, 0:8])
                    nc.scalar.copy(
                        out=res[a][:, H:H + 7, :],
                        in_=half[1][:, 9:9 + 7 * PITCH].rearrange("p (r q) -> p r q", q=PITCH)[:, ::-1, 0:W],
                    )
                    nc.sync.dma_start(
                        out=out[1, P * a:P * (a + 1), 0:8, :].rearrange("o h w -> o (h w)"),
                        in_=res[a][:, H:H + 8, :].rearrange("p r w -> p (r w)"),
                    )

        ctx.enter_context(tc.manual_schedule())
        load_w(0)
        load_x(0)
        load_w(1)
        load_w(2)
        load_w(3)
        load_x(1)
        zeros()
        x_quant(576, 64)
        w_split(0, "v")
        w_turn(0)
        warm_up(4)
        x_group(0)
        w_split(1, "s")
        w_quant(0)
        x_quant(0, 512)
        x_quant(512, 64)
        x_plane(0, 512)
        product(0, 0, "s")
        w_turn(1)
        w_split(2, "v")
        w_turn(2)
        warm_up(2)
        w_split(3, "v")
        w_turn(3)
        warm_up(3)
        x_group(1)
        w_quant(1)
        product(1, 0, "s")
        x_quant(640, 512)
        x_quant(1152, 64)
        x_plane(512, 1152)
        w_quant(2)
        w_quant(3)
        product(0, 1, "v")
        product(0, 2, "v")
        product(1, 1, "v")
        product(1, 2, "s")
        product(2, 0, "v")
        product(2, 1, "v")
        product(2, 2, "s")
        product(3, 0, "v")
        product(3, 1, "v")
        last_product(3)
